import numpy as np
import ml_dtypes


def mxq(x, axis, fmt="e4m3"):
    dtype, down = {"e4m3": (ml_dtypes.float8_e4m3fn, 7), "e5m2": (ml_dtypes.float8_e5m2, 14)}[fmt]
    v = np.moveaxis(np.asarray(x, np.float32).astype(ml_dtypes.bfloat16).astype(np.float64), axis, -1)
    blocks = v.reshape(v.shape[:-1] + (-1, 32))
    amax = np.abs(blocks).max(-1, keepdims=True)
    byte = np.maximum(np.where(amax > 0, np.frexp(amax)[1] - 1 + 127, 0) - down, 1)
    scale = np.exp2(byte - 127.0)
    codes = (blocks / scale).astype(np.float32).astype(dtype).astype(np.float64)
    return np.moveaxis((codes * scale).reshape(v.shape), -1, axis)


WIDE = False


def mx_kscale(k):
    if not WIDE:
        return np.ones(k)
    levels = np.array([10, -10, 5, -5, 0])
    if k % 512:
        return np.exp2(np.random.permutation(np.resize(levels, k // 32))).repeat(32)
    a = np.empty((k // 512, 16))
    for p in range(k // 512):
        a[p, :8] = np.random.permutation(np.resize(levels, 8))
        for g in range(8):
            far = levels[np.abs(levels - a[p, g]) >= 10]
            a[p, g + 8] = far[np.random.randint(len(far))]
    return np.exp2(a.ravel()).repeat(32)


BF16 = ml_dtypes.bfloat16


def bf(x):
    return np.asarray(x, np.float32).astype(BF16)


def f64(x):
    return np.asarray(x).astype(np.float64)


N, E, C = 2048, 1024, 512
DENSITY = 0.01


def setup_inputs():
    s, t = mx_kscale(N), mx_kscale(C)
    member = np.random.uniform(size=(N, E)) < DENSITY
    return {"node_features": bf(np.random.standard_normal((N, C)) / s[:, None] * t[None, :]),
            "incidence": bf(member * s[:, None]),
            "W1": bf(np.random.standard_normal((C, C)) * np.sqrt(E) / np.sqrt(DENSITY * N * C) / t[:, None]),
            "b1": bf(np.random.standard_normal(C) * 0.1 * np.sqrt(E)),
            "edge_attention": bf(1.0 + np.random.standard_normal(E))}


def reference(node_features, incidence, W1, b1, edge_attention):
    agg = mxq(f64(incidence), 0, "e4m3").T @ mxq(f64(node_features), 0, "e4m3")
    lin = (mxq(agg, 1, "e4m3") @ mxq(f64(W1), 0, "e4m3")) + f64(b1)
    a = f64(edge_attention)
    e = np.exp(a - a.max())
    attn = e / e.sum()
    return lin * attn[:, None]

@@ -1,0 +1,292 @@
+import concourse.mybir as mybir
+from concourse.masks import make_identity
+
+BF16 = mybir.dt.bfloat16
+F32 = mybir.dt.float32
+U32 = mybir.dt.uint32
+U8 = mybir.dt.uint8
+FP8X4 = mybir.dt.float8_e4m3fn_x4
+ALU = mybir.AluOpType
+ACT = mybir.ActivationFunctionType
+AXIS = mybir.AxisListType
+
+N_NODES, N_EDGES, N_CH = 2048, 1024, 512
+
+P = 128
+PACK = 4
+K_PASS = P * PACK
+WIDTH = 512
+NODE_PASSES = N_NODES // K_PASS
+CH_TILES = N_CH // P
+EDGE_TILES = N_EDGES // P
+HALVES = N_EDGES // WIDTH
+HALF = WIDTH // P
+RUN = 4
+SCALAR_COLS = 256
+
+FLOPS = 2 * N_EDGES * N_NODES * N_CH + 2 * N_EDGES * N_CH * N_CH
+
+assert CH_TILES == PACK and N_CH == WIDTH
+
+
+def tile_heterogeneoustemporalhypergraphnn_pa_kernel(
+    tc, node_features, incidence, W1, b1, edge_attention, out
+):
+    nc = tc.nc
+
+    with tc.tile_pool(name="chunks", bufs=1) as chunk_pool, tc.tile_pool(
+        name="agg", bufs=1
+    ) as agg_pool, tc.tile_pool(name="small", bufs=1) as small_pool, tc.tile_pool(
+        name="result", bufs=4
+    ) as result_pool:
+
+        def load_chunk(name, rows_of_partition):
+            chunk = {
+                "rows": chunk_pool.tile([P, PACK, WIDTH], BF16, name=name + "_rows"),
+                "grouped": chunk_pool.tile(
+                    [P, WIDTH, PACK], BF16, align_bytes=64, name=name + "_grouped"
+                ),
+                "codes": chunk_pool.tile([P, WIDTH], U32, align_bytes=64, name=name + "_codes"),
+                "scales": chunk_pool.tile([P, WIDTH], U8, align_bytes=64, name=name + "_scales"),
+            }
+            nc.sync.dma_start(out=chunk["rows"][:], in_=rows_of_partition)
+            return chunk
+
+        def regroup_columns(copy, chunk, cols):
+            copy(
+                out=chunk["grouped"][:, cols, :].rearrange("p (c i) j -> p c j i", i=RUN),
+                in_=chunk["rows"][:, :, cols].rearrange("p j (c i) -> p c j i", i=RUN),
+            )
+
+        def regroup_channels(copy, chunk, ms):
+            copy(
+                out=chunk["grouped"][:].rearrange("p (t m) j -> p m j t", t=PACK)[:, ms],
+                in_=chunk["rows"][:].rearrange("p j (m t) -> p m j t", t=PACK)[:, ms],
+            )
+
+        def regroup_nf(chunk):
+            regroup_channels(nc.scalar.copy, chunk, slice(0, SCALAR_COLS // PACK))
+            regroup_channels(nc.vector.tensor_copy, chunk, slice(SCALAR_COLS // PACK, P))
+
+        def regroup(chunk):
+            regroup_columns(nc.scalar.copy, chunk, slice(0, SCALAR_COLS))
+            regroup_columns(nc.vector.tensor_copy, chunk, slice(SCALAR_COLS, WIDTH))
+
+        def quantise(chunk):
+            nc.vector.quantize_mx(
+                out=chunk["codes"][:].bitcast(FP8X4),
+                scales=chunk["scales"][:],
+                in_=chunk["grouped"][:].rearrange("p w j -> p (w j)"),
+            )
+
+        logit_rows = small_pool.tile([P, P], BF16)
+        bias_rows = small_pool.tile([P, N_CH], BF16)
+        ones_bf = small_pool.tile([P, P], BF16)
+        ones_f32 = small_pool.tile([P, P], F32)
+        ident_bf = small_pool.tile([P, P], BF16)
+        table_warm = small_pool.tile([P, 1], F32)
+        nc.gpsimd.memset(logit_rows[:], 0.0)
+        nc.gpsimd.memset(bias_rows[:], 0.0)
+        nc.vector.memset(table_warm[:], 0.0)
+        nc.vector.memset(ones_bf[:], 1.0)
+        nc.vector.memset(ones_f32[:], 1.0)
+        make_identity(nc, ident_bf[:])
+        nc.scalar.activation(out=table_warm[:], in_=table_warm[:], func=ACT.Exp)
+
+        nc.sync.dma_start(
+            out=logit_rows[0:EDGE_TILES, :],
+            in_=edge_attention.rearrange("(i q) -> i q", q=P),
+        )
+        nf = [
+            load_chunk(
+                "nf%d" % c,
+                node_features[c * K_PASS : (c + 1) * K_PASS, :].rearrange("(p j) w -> p j w", j=PACK),
+            )
+            for c in range(NODE_PASSES)
+        ]
+        nc.sync.dma_start(out=bias_rows[0:1, :], in_=b1.rearrange("(o n) -> o n", o=1))
+        inc = [
+            [
+                load_chunk(
+                    "inc%d_%d" % (h, c),
+                    incidence[c * K_PASS : (c + 1) * K_PASS, h * WIDTH : (h + 1) * WIDTH].rearrange(
+                        "(p j) w -> p j w", j=PACK
+                    ),
+                )
+                for c in range(NODE_PASSES)
+            ]
+            for h in range(HALVES)
+        ]
+        w1 = load_chunk("w1", W1.rearrange("(p t) n -> p t n", t=PACK))
+
+        logit_col = small_pool.tile([P, EDGE_TILES], F32)
+        part_max = small_pool.tile([P, 1], F32)
+        part_max_bf = small_pool.tile([P, 1], BF16)
+        all_max = small_pool.tile([P, 1], F32)
+        shifted = small_pool.tile([P, EDGE_TILES], F32)
+        exp_col = small_pool.tile([P, EDGE_TILES], F32)
+        exp_sum = small_pool.tile([P, 1], F32)
+        inv_sum = small_pool.tile([P, 1], F32)
+        attn_col = small_pool.tile([P, EDGE_TILES], F32)
+
+        def softmax_partial_max():
+            nc.tensor.transpose(logit_ps[:], logit_rows[:], ident_bf[:])
+            nc.vector.tensor_copy(out=logit_col[:], in_=logit_ps[:, 0:EDGE_TILES])
+            nc.vector.tensor_reduce(out=part_max[:], in_=logit_col[:], axis=AXIS.X, op=ALU.max)
+            nc.vector.tensor_copy(out=part_max_bf[:], in_=part_max[:])
+            nc.tensor.matmul(
+                out=max_ps[:],
+                lhsT=part_max_bf[:, 0:1].to_broadcast([P, P]),
+                rhs=ident_bf[:],
+                start=True,
+                stop=True,
+            )
+
+        def softmax_exp():
+            nc.vector.tensor_reduce(out=all_max[:], in_=max_ps[:], axis=AXIS.X, op=ALU.max)
+            nc.vector.tensor_scalar(
+                out=shifted[:],
+                in0=logit_col[:],
+                scalar1=all_max[:, 0:1],
+                scalar2=None,
+                op0=ALU.subtract,
+            )
+            nc.scalar.activation(out=exp_col[:], in_=shifted[:], func=ACT.Exp)
+            nc.tensor.matmul(out=sum_ps[:], lhsT=ones_f32[:], rhs=exp_col[:], start=True, stop=True)
+
+        def softmax_normalise():
+            nc.vector.tensor_reduce(out=exp_sum[:], in_=sum_ps[:], axis=AXIS.X, op=ALU.add)
+            nc.vector.reciprocal(out=inv_sum[:], in_=exp_sum[:])
+            nc.vector.tensor_scalar(
+                out=attn_col[:],
+                in0=exp_col[:],
+                scalar1=inv_sum[:, 0:1],
+                scalar2=None,
+                op0=ALU.mult,
+            )
+
+        bias_all = small_pool.tile([P, N_CH], F32)
+        bias_attn = small_pool.tile([P, EDGE_TILES, N_CH], F32)
+
+        def spread_bias():
+            nc.tensor.matmul(out=bias_ps[:], lhsT=ones_bf[:], rhs=bias_rows[:], start=True, stop=True)
+            nc.scalar.copy(out=bias_all[:], in_=bias_ps[:])
+
+        def scale_bias(i):
+            nc.gpsimd.tensor_scalar(
+                out=bias_attn[:, i, :],
+                in0=bias_all[:],
+                scalar1=attn_col[:, i : i + 1],
+                scalar2=0.0,
+                op0=ALU.mult,
+                op1=ALU.add,
+            )
+
+        agg_grouped = agg_pool.tile([P, EDGE_TILES, P, PACK], BF16, align_bytes=64)
+        agg_codes = agg_pool.tile([P, EDGE_TILES, P], U32, align_bytes=64)
+        agg_scales = agg_pool.tile([P, EDGE_TILES, P], U8, align_bytes=64)
+        agg_banks = {}
+        lin_banks = {}
+
+        def aggregate(i):
+            half = inc[i // HALF]
+            edges = slice((i % HALF) * P, (i % HALF + 1) * P)
+            agg_banks[i] = main_psum.tile([P, CH_TILES, P], F32, tag="agg", name="agg_ps%d" % i)
+            for t in range(CH_TILES):
+                channels = slice(t * P, (t + 1) * P)
+                for c in range(NODE_PASSES):
+                    nc.tensor.matmul_mx(
+                        out=agg_banks[i][:, t, :],
+                        lhsT=nf[c]["codes"][:, channels].bitcast(FP8X4),
+                        lhsT_scale=nf[c]["scales"][:, channels],
+                        rhs=half[c]["codes"][:, edges].bitcast(FP8X4),
+                        rhs_scale=half[c]["scales"][:, edges],
+                        start=(c == 0),
+                        stop=(c == NODE_PASSES - 1),
+                    )
+
+        def round_agg(i):
+            nc.scalar.copy(out=agg_grouped[:, i], in_=agg_banks[i][:].rearrange("p t e -> p e t"))
+
+        def quantise_agg(i):
+            nc.vector.quantize_mx(
+                out=agg_codes[:, i, :].bitcast(FP8X4),
+                scales=agg_scales[:, i, :],
+                in_=agg_grouped[:, i].rearrange("p e t -> p (e t)"),
+            )
+
+        def project(i):
+            lin_banks[i] = main_psum.tile([P, N_CH], F32, tag="lin", name="lin_ps%d" % i)
+            nc.tensor.matmul_mx(
+                out=lin_banks[i][:],
+                lhsT=agg_codes[:, i, :].bitcast(FP8X4),
+                lhsT_scale=agg_scales[:, i, :],
+                rhs=w1["codes"][:].bitcast(FP8X4),
+                rhs_scale=w1["scales"][:],
+                start=True,
+                stop=True,
+            )
+
+        def finish(i):
+            result = result_pool.tile([P, N_CH], F32)
+            nc.vector.scalar_tensor_tensor(
+                out=result[:],
+                in0=lin_banks[i][:],
+                scalar=attn_col[:, i : i + 1],
+                in1=bias_attn[:, i, :],
+                op0=ALU.mult,
+                op1=ALU.add,
+            )
+            nc.sync.dma_start(out=out[i * P : (i + 1) * P, :], in_=result[:])
+
+        with tc.psum_pool(name="setup_psum", bufs=1) as setup_psum:
+            logit_ps = setup_psum.tile([P, P], BF16)
+            max_ps = setup_psum.tile([P, P], F32)
+            sum_ps = setup_psum.tile([P, EDGE_TILES], F32)
+            bias_ps = setup_psum.tile([P, N_CH], F32)
+            softmax_partial_max()
+            softmax_exp()
+            regroup_nf(nf[0])
+            softmax_normalise()
+            for c in range(1, NODE_PASSES):
+                regroup_nf(nf[c])
+                quantise(nf[c - 1])
+            spread_bias()
+        for i in range(EDGE_TILES):
+            scale_bias(i)
+
+        with tc.psum_pool(name="main_psum", bufs=HALF) as main_psum:
+            regroup(inc[0][0])
+            quantise(nf[3])
+            for c in range(1, NODE_PASSES):
+                regroup(inc[0][c])
+                quantise(inc[0][c - 1])
+            quantise(inc[0][NODE_PASSES - 1])
+            for i in range(HALF):
+                aggregate(i)
+            regroup(inc[1][0])
+            for c in range(1, NODE_PASSES):
+                regroup(inc[1][c])
+                quantise(inc[1][c - 1])
+            quantise(inc[1][NODE_PASSES - 1])
+            for i in range(HALF // 2):
+                round_agg(i)
+                aggregate(HALF + i)
+            regroup(w1)
+            for i in range(HALF // 2):
+                quantise_agg(i)
+            quantise(w1)
+            for i in range(HALF // 2, HALF):
+                round_agg(i)
+                quantise_agg(i)
+            for i in range(HALF):
+                project(i)
+            aggregate(HALF + 2)
+            aggregate(HALF + 3)
+            for i in range(HALF):
+                finish(i)
+                round_agg(HALF + i)
+                quantise_agg(HALF + i)
+                project(HALF + i)
+            for i in range(HALF, EDGE_TILES):
+                finish(i)

@@ -23,6 +23,8 @@ HALVES = N_EDGES // WIDTH
 HALF = WIDTH // P
 RUN = 4
 SCALAR_COLS = 256
+AGG_BANKS = 6
+LIN_BANKS = 2
 
 FLOPS = 2 * N_EDGES * N_NODES * N_CH + 2 * N_EDGES * N_CH * N_CH
 
@@ -84,91 +86,67 @@ def tile_heterogeneoustemporalhypergraphnn_pa_kernel(
         ones_bf = small_pool.tile([P, P], BF16)
         ones_f32 = small_pool.tile([P, P], F32)
         ident_bf = small_pool.tile([P, P], BF16)
+        neg_ident = small_pool.tile([P, P], BF16)
         table_warm = small_pool.tile([P, 1], F32)
-        nc.gpsimd.memset(logit_rows[:], 0.0)
-        nc.gpsimd.memset(bias_rows[:], 0.0)
-        nc.vector.memset(table_warm[:], 0.0)
-        nc.vector.memset(ones_bf[:], 1.0)
-        nc.vector.memset(ones_f32[:], 1.0)
-        make_identity(nc, ident_bf[:])
-        nc.scalar.activation(out=table_warm[:], in_=table_warm[:], func=ACT.Exp)
 
-        nc.sync.dma_start(
-            out=logit_rows[0:EDGE_TILES, :],
-            in_=edge_attention.rearrange("(i q) -> i q", q=P),
-        )
-        nf = [
-            load_chunk(
-                "nf%d" % c,
-                node_features[c * K_PASS : (c + 1) * K_PASS, :].rearrange("(p j) w -> p j w", j=PACK),
-            )
-            for c in range(NODE_PASSES)
-        ]
-        nc.sync.dma_start(out=bias_rows[0:1, :], in_=b1.rearrange("(o n) -> o n", o=1))
-        inc = [
-            [
-                load_chunk(
-                    "inc%d_%d" % (h, c),
-                    incidence[c * K_PASS : (c + 1) * K_PASS, h * WIDTH : (h + 1) * WIDTH].rearrange(
-                        "(p j) w -> p j w", j=PACK
-                    ),
-                )
-                for c in range(NODE_PASSES)
-            ]
-            for h in range(HALVES)
-        ]
-        w1 = load_chunk("w1", W1.rearrange("(p t) n -> p t n", t=PACK))
-
-        logit_col = small_pool.tile([P, EDGE_TILES], F32)
-        part_max = small_pool.tile([P, 1], F32)
         part_max_bf = small_pool.tile([P, 1], BF16)
-        all_max = small_pool.tile([P, 1], F32)
-        shifted = small_pool.tile([P, EDGE_TILES], F32)
+        neg_max = small_pool.tile([P, 1], F32)
         exp_col = small_pool.tile([P, EDGE_TILES], F32)
-        exp_sum = small_pool.tile([P, 1], F32)
+        exp_part = small_pool.tile([P, 1], F32)
         inv_sum = small_pool.tile([P, 1], F32)
         attn_col = small_pool.tile([P, EDGE_TILES], F32)
+        setup_banks = {}
 
         def softmax_partial_max():
+            logit_ps = main_psum.tile([P, P], BF16, tag="lin", name="logit_ps")
+            setup_banks["logits"] = logit_ps[:, 0:EDGE_TILES]
             nc.tensor.transpose(logit_ps[:], logit_rows[:], ident_bf[:])
-            nc.vector.tensor_copy(out=logit_col[:], in_=logit_ps[:, 0:EDGE_TILES])
-            nc.vector.tensor_reduce(out=part_max[:], in_=logit_col[:], axis=AXIS.X, op=ALU.max)
-            nc.vector.tensor_copy(out=part_max_bf[:], in_=part_max[:])
+            nc.vector.tensor_reduce(
+                out=part_max_bf[:], in_=setup_banks["logits"], axis=AXIS.X, op=ALU.max
+            )
+            max_ps = main_psum.tile([P, P], F32, tag="lin", name="max_ps")
+            setup_banks["max"] = max_ps
             nc.tensor.matmul(
                 out=max_ps[:],
                 lhsT=part_max_bf[:, 0:1].to_broadcast([P, P]),
-                rhs=ident_bf[:],
+                rhs=neg_ident[:],
                 start=True,
                 stop=True,
             )
 
         def softmax_exp():
-            nc.vector.tensor_reduce(out=all_max[:], in_=max_ps[:], axis=AXIS.X, op=ALU.max)
-            nc.vector.tensor_scalar(
-                out=shifted[:],
-                in0=logit_col[:],
-                scalar1=all_max[:, 0:1],
-                scalar2=None,
-                op0=ALU.subtract,
+            nc.vector.tensor_reduce(
+                out=neg_max[:], in_=setup_banks["max"][:], axis=AXIS.X, op=ALU.min
             )
-            nc.scalar.activation(out=exp_col[:], in_=shifted[:], func=ACT.Exp)
-            nc.tensor.matmul(out=sum_ps[:], lhsT=ones_f32[:], rhs=exp_col[:], start=True, stop=True)
+            nc.scalar.activation(
+                out=exp_col[:],
+                in_=setup_banks["logits"],
+                func=ACT.Exp,
+                bias=neg_max[:, 0:1],
+                accum_out=exp_part[:],
+            )
+
+        def softmax_sum():
+            sum_ps = main_psum.tile([P, 1], F32, tag="lin", name="sum_ps")
+            setup_banks["sum"] = sum_ps
+            nc.tensor.matmul(out=sum_ps[:], lhsT=ones_f32[:], rhs=exp_part[:], start=True, stop=True)
 
         def softmax_normalise():
-            nc.vector.tensor_reduce(out=exp_sum[:], in_=sum_ps[:], axis=AXIS.X, op=ALU.add)
-            nc.vector.reciprocal(out=inv_sum[:], in_=exp_sum[:])
-            nc.vector.tensor_scalar(
+            nc.vector.reciprocal(out=inv_sum[:], in_=setup_banks["sum"][:])
+            nc.gpsimd.tensor_scalar(
                 out=attn_col[:],
                 in0=exp_col[:],
                 scalar1=inv_sum[:, 0:1],
-                scalar2=None,
+                scalar2=0.0,
                 op0=ALU.mult,
+                op1=ALU.add,
             )
 
         bias_all = small_pool.tile([P, N_CH], F32)
         bias_attn = small_pool.tile([P, EDGE_TILES, N_CH], F32)
 
         def spread_bias():
+            bias_ps = main_psum.tile([P, N_CH], F32, tag="lin", name="bias_ps")
             nc.tensor.matmul(out=bias_ps[:], lhsT=ones_bf[:], rhs=bias_rows[:], start=True, stop=True)
             nc.scalar.copy(out=bias_all[:], in_=bias_ps[:])
 
@@ -188,22 +166,32 @@ def tile_heterogeneoustemporalhypergraphnn_pa_kernel(
         agg_banks = {}
         lin_banks = {}
 
-        def aggregate(i):
-            half = inc[i // HALF]
-            edges = slice((i % HALF) * P, (i % HALF + 1) * P)
-            agg_banks[i] = main_psum.tile([P, CH_TILES, P], F32, tag="agg", name="agg_ps%d" % i)
-            for t in range(CH_TILES):
-                channels = slice(t * P, (t + 1) * P)
-                for c in range(NODE_PASSES):
+        def aggregate(h, c):
+            for e in range(HALF):
+                i = h * HALF + e
+                if c == 0:
+                    agg_banks[i] = main_psum.tile(
+                        [P, CH_TILES, P], F32, tag="agg", name="agg_ps%d" % i, bufs=AGG_BANKS
+                    )
+                edges = slice(e * P, (e + 1) * P)
+                for t in range(CH_TILES):
+                    channels = slice(t * P, (t + 1) * P)
                     nc.tensor.matmul_mx(
                         out=agg_banks[i][:, t, :],
                         lhsT=nf[c]["codes"][:, channels].bitcast(FP8X4),
                         lhsT_scale=nf[c]["scales"][:, channels],
-                        rhs=half[c]["codes"][:, edges].bitcast(FP8X4),
-                        rhs_scale=half[c]["scales"][:, edges],
-                        start=(c == 0),
-                        stop=(c == NODE_PASSES - 1),
+                        rhs=inc[h][c]["codes"][:, edges].bitcast(FP8X4),
+                        rhs_scale=inc[h][c]["scales"][:, edges],
+                        start=(c == 0 and t == 0),
+                        stop=(c == NODE_PASSES - 1 and t == CH_TILES - 1),
                     )
+
+        def warm_tensor(chunk):
+            for j in range(2):
+                scratch = main_psum.tile([P, WIDTH], F32, tag="lin", name="scratch")
+                nc.tensor.matmul(
+                    out=scratch[:], lhsT=ones_bf[:], rhs=chunk["rows"][:, j, :], start=True, stop=True
+                )
 
         def round_agg(i):
             nc.scalar.copy(out=agg_grouped[:, i], in_=agg_banks[i][:].rearrange("p t e -> p e t"))
@@ -239,54 +227,95 @@ def tile_heterogeneoustemporalhypergraphnn_pa_kernel(
             )
             nc.sync.dma_start(out=out[i * P : (i + 1) * P, :], in_=result[:])
 
-        with tc.psum_pool(name="setup_psum", bufs=1) as setup_psum:
-            logit_ps = setup_psum.tile([P, P], BF16)
-            max_ps = setup_psum.tile([P, P], F32)
-            sum_ps = setup_psum.tile([P, EDGE_TILES], F32)
-            bias_ps = setup_psum.tile([P, N_CH], F32)
-            softmax_partial_max()
-            softmax_exp()
-            regroup_nf(nf[0])
-            softmax_normalise()
-            for c in range(1, NODE_PASSES):
-                regroup_nf(nf[c])
-                quantise(nf[c - 1])
-            spread_bias()
-        for i in range(EDGE_TILES):
-            scale_bias(i)
+        with tc.psum_pool(name="main_psum", bufs=LIN_BANKS) as main_psum, tc.manual_schedule():
+            nc.vector.memset(table_warm[:], 0.0)
+            nc.vector.memset(logit_rows[:], 0.0)
+            nc.vector.memset(bias_rows[:], 0.0)
+            nc.vector.memset(ones_bf[:], 1.0)
+            nc.vector.memset(ones_f32[:], 1.0)
+            make_identity(nc, ident_bf[:])
+            nc.gpsimd.tensor_scalar(
+                out=neg_ident[:], in0=ident_bf[:], scalar1=-1.0, scalar2=0.0, op0=ALU.mult, op1=ALU.add
+            )
+            nc.scalar.activation(out=table_warm[:], in_=table_warm[:], func=ACT.Exp)
 
-        with tc.psum_pool(name="main_psum", bufs=HALF) as main_psum:
+            def load_nf(c):
+                return load_chunk(
+                    "nf%d" % c,
+                    node_features[c * K_PASS : (c + 1) * K_PASS, :].rearrange("(p j) w -> p j w", j=PACK),
+                )
+
+            def load_inc(h):
+                return [
+                    load_chunk(
+                        "inc%d_%d" % (h, c),
+                        incidence[c * K_PASS : (c + 1) * K_PASS, h * WIDTH : (h + 1) * WIDTH].rearrange(
+                            "(p j) w -> p j w", j=PACK
+                        ),
+                    )
+                    for c in range(NODE_PASSES)
+                ]
+
+            nf = [load_nf(0)]
+            nc.sync.dma_start(
+                out=logit_rows[0:EDGE_TILES, :],
+                in_=edge_attention.rearrange("(i q) -> i q", q=P),
+            )
+            nf += [load_nf(c) for c in range(1, NODE_PASSES)]
+            nc.sync.dma_start(out=bias_rows[0:1, :], in_=b1.rearrange("(o n) -> o n", o=1))
+            inc = [load_inc(0)]
+            w1 = load_chunk("w1", W1.rearrange("(p t) n -> p t n", t=PACK))
+            inc.append(load_inc(1))
+
+            regroup_nf(nf[0])
+            regroup_nf(nf[1])
+            quantise(nf[0])
+            softmax_partial_max()
+            regroup_nf(nf[2])
+            quantise(nf[1])
+            softmax_exp()
+            softmax_sum()
+            regroup_nf(nf[3])
+            quantise(nf[2])
+            softmax_normalise()
+            spread_bias()
+            for i in range(EDGE_TILES):
+                scale_bias(i)
+            warm_tensor(inc[0][0])
             regroup(inc[0][0])
             quantise(nf[3])
+            warm_tensor(inc[0][1])
+            warm_tensor(inc[0][2])
             for c in range(1, NODE_PASSES):
                 regroup(inc[0][c])
                 quantise(inc[0][c - 1])
+                aggregate(0, c - 1)
+            regroup(w1)
             quantise(inc[0][NODE_PASSES - 1])
-            for i in range(HALF):
-                aggregate(i)
+            aggregate(0, NODE_PASSES - 1)
             regroup(inc[1][0])
+            quantise(w1)
+            round_agg(0)
             for c in range(1, NODE_PASSES):
                 regroup(inc[1][c])
+                quantise_agg(c - 1)
+                project(c - 1)
+                round_agg(c)
                 quantise(inc[1][c - 1])
+                aggregate(1, c - 1)
+                if c > 1:
+                    finish(c - 2)
+            quantise_agg(HALF - 1)
+            project(HALF - 1)
             quantise(inc[1][NODE_PASSES - 1])
-            for i in range(HALF // 2):
-                round_agg(i)
-                aggregate(HALF + i)
-            regroup(w1)
-            for i in range(HALF // 2):
-                quantise_agg(i)
-            quantise(w1)
-            for i in range(HALF // 2, HALF):
-                round_agg(i)
-                quantise_agg(i)
-            for i in range(HALF):
-                project(i)
-            aggregate(HALF + 2)
-            aggregate(HALF + 3)
-            for i in range(HALF):
-                finish(i)
-                round_agg(HALF + i)
-                quantise_agg(HALF + i)
-                project(HALF + i)
+            aggregate(1, NODE_PASSES - 1)
             for i in range(HALF, EDGE_TILES):
-                finish(i)
+                round_agg(i)
+            finish(HALF - 2)
+            finish(HALF - 1)
+            for i in range(HALF, EDGE_TILES):
+                quantise_agg(i)
+                project(i)
+                if i > HALF:
+                    finish(i - 1)
+            finish(EDGE_TILES - 1)

@@ -114,10 +114,12 @@ def tile_heterogeneoustemporalhypergraphnn_pa_kernel(
                 stop=True,
             )
 
-        def softmax_exp():
+        def softmax_max():
             nc.vector.tensor_reduce(
                 out=neg_max[:], in_=setup_banks["max"][:], axis=AXIS.X, op=ALU.min
             )
+
+        def softmax_exp():
             nc.scalar.activation(
                 out=exp_col[:],
                 in_=setup_banks["logits"],
@@ -151,13 +153,12 @@ def tile_heterogeneoustemporalhypergraphnn_pa_kernel(
             nc.scalar.copy(out=bias_all[:], in_=bias_ps[:])
 
         def scale_bias(i):
-            nc.gpsimd.tensor_scalar(
+            nc.vector.tensor_scalar(
                 out=bias_attn[:, i, :],
                 in0=bias_all[:],
                 scalar1=attn_col[:, i : i + 1],
-                scalar2=0.0,
+                scalar2=None,
                 op0=ALU.mult,
-                op1=ALU.add,
             )
 
         agg_grouped = agg_pool.tile([P, EDGE_TILES, P, PACK], BF16, align_bytes=64)
@@ -273,16 +274,15 @@ def tile_heterogeneoustemporalhypergraphnn_pa_kernel(
             softmax_partial_max()
             regroup_nf(nf[2])
             quantise(nf[1])
+            softmax_max()
+            regroup_nf(nf[3])
             softmax_exp()
             softmax_sum()
-            regroup_nf(nf[3])
             quantise(nf[2])
-            softmax_normalise()
-            spread_bias()
-            for i in range(EDGE_TILES):
-                scale_bias(i)
             warm_tensor(inc[0][0])
             regroup(inc[0][0])
+            spread_bias()
+            softmax_normalise()
             quantise(nf[3])
             warm_tensor(inc[0][1])
             warm_tensor(inc[0][2])
@@ -295,9 +295,11 @@ def tile_heterogeneoustemporalhypergraphnn_pa_kernel(
             aggregate(0, NODE_PASSES - 1)
             regroup(inc[1][0])
             quantise(w1)
+            scale_bias(0)
             round_agg(0)
             for c in range(1, NODE_PASSES):
                 regroup(inc[1][c])
+                scale_bias(c)
                 quantise_agg(c - 1)
                 project(c - 1)
                 round_agg(c)
@@ -313,6 +315,8 @@ def tile_heterogeneoustemporalhypergraphnn_pa_kernel(
                 round_agg(i)
             finish(HALF - 2)
             finish(HALF - 1)
+            for i in range(HALF, EDGE_TILES):
+                scale_bias(i)
             for i in range(HALF, EDGE_TILES):
                 quantise_agg(i)
                 project(i)

@@ -150,9 +150,17 @@ def tile_heterogeneoustemporalhypergraphnn_pa_kernel(
         def spread_bias():
             bias_ps = main_psum.tile([P, N_CH], F32, tag="lin", name="bias_ps")
             nc.tensor.matmul(out=bias_ps[:], lhsT=ones_bf[:], rhs=bias_rows[:], start=True, stop=True)
-            nc.scalar.copy(out=bias_all[:], in_=bias_ps[:])
+            setup_banks["bias"] = bias_ps
 
-        def scale_bias(i):
+        def keep_bias():
+            nc.scalar.copy(out=bias_all[:], in_=setup_banks["bias"][:])
+
+        def scale_bias_on_scalar(i):
+            nc.scalar.activation(
+                out=bias_attn[:, i, :], in_=bias_all[:], func=ACT.Copy, scale=attn_col[:, i : i + 1]
+            )
+
+        def scale_bias_on_vector(i):
             nc.vector.tensor_scalar(
                 out=bias_attn[:, i, :],
                 in0=bias_all[:],
@@ -277,12 +285,13 @@ def tile_heterogeneoustemporalhypergraphnn_pa_kernel(
             softmax_max()
             regroup_nf(nf[3])
             softmax_exp()
+            spread_bias()
             softmax_sum()
             quantise(nf[2])
-            warm_tensor(inc[0][0])
             regroup(inc[0][0])
-            spread_bias()
+            keep_bias()
             softmax_normalise()
+            warm_tensor(inc[0][0])
             quantise(nf[3])
             warm_tensor(inc[0][1])
             warm_tensor(inc[0][2])
@@ -290,16 +299,18 @@ def tile_heterogeneoustemporalhypergraphnn_pa_kernel(
                 regroup(inc[0][c])
                 quantise(inc[0][c - 1])
                 aggregate(0, c - 1)
+                if c > 1:
+                    scale_bias_on_vector(c)
             regroup(w1)
             quantise(inc[0][NODE_PASSES - 1])
             aggregate(0, NODE_PASSES - 1)
             regroup(inc[1][0])
             quantise(w1)
-            scale_bias(0)
+            scale_bias_on_scalar(0)
+            scale_bias_on_scalar(1)
             round_agg(0)
             for c in range(1, NODE_PASSES):
                 regroup(inc[1][c])
-                scale_bias(c)
                 quantise_agg(c - 1)
                 project(c - 1)
                 round_agg(c)
@@ -311,12 +322,14 @@ def tile_heterogeneoustemporalhypergraphnn_pa_kernel(
             project(HALF - 1)
             quantise(inc[1][NODE_PASSES - 1])
             aggregate(1, NODE_PASSES - 1)
+            for i in range(HALF, EDGE_TILES - 1):
+                scale_bias_on_scalar(i)
             for i in range(HALF, EDGE_TILES):
+                if i == EDGE_TILES - 1:
+                    scale_bias_on_scalar(i)
                 round_agg(i)
             finish(HALF - 2)
             finish(HALF - 1)
-            for i in range(HALF, EDGE_TILES):
-                scale_bias(i)
             for i in range(HALF, EDGE_TILES):
                 quantise_agg(i)
                 project(i)

import concourse.mybir as mybir
from concourse.masks import make_identity

BF16 = mybir.dt.bfloat16
F32 = mybir.dt.float32
U32 = mybir.dt.uint32
U8 = mybir.dt.uint8
FP8X4 = mybir.dt.float8_e4m3fn_x4
ALU = mybir.AluOpType
ACT = mybir.ActivationFunctionType
AXIS = mybir.AxisListType

N_NODES, N_EDGES, N_CH = 2048, 1024, 512

P = 128
PACK = 4
K_PASS = P * PACK
WIDTH = 512
NODE_PASSES = N_NODES // K_PASS
CH_TILES = N_CH // P
EDGE_TILES = N_EDGES // P
HALVES = N_EDGES // WIDTH
HALF = WIDTH // P
RUN = 4
SCALAR_COLS = 256
AGG_BANKS = 6
LIN_BANKS = 2

FLOPS = 2 * N_EDGES * N_NODES * N_CH + 2 * N_EDGES * N_CH * N_CH

assert CH_TILES == PACK and N_CH == WIDTH


def tile_heterogeneoustemporalhypergraphnn_pa_kernel(
    tc, node_features, incidence, W1, b1, edge_attention, out
):
    nc = tc.nc

    with tc.tile_pool(name="chunks", bufs=1) as chunk_pool, tc.tile_pool(
        name="agg", bufs=1
    ) as agg_pool, tc.tile_pool(name="small", bufs=1) as small_pool, tc.tile_pool(
        name="result", bufs=4
    ) as result_pool:

        def load_chunk(name, rows_of_partition):
            chunk = {
                "rows": chunk_pool.tile([P, PACK, WIDTH], BF16, name=name + "_rows"),
                "grouped": chunk_pool.tile(
                    [P, WIDTH, PACK], BF16, align_bytes=64, name=name + "_grouped"
                ),
                "codes": chunk_pool.tile([P, WIDTH], U32, align_bytes=64, name=name + "_codes"),
                "scales": chunk_pool.tile([P, WIDTH], U8, align_bytes=64, name=name + "_scales"),
            }
            nc.sync.dma_start(out=chunk["rows"][:], in_=rows_of_partition)
            return chunk

        def regroup_columns(copy, chunk, cols):
            copy(
                out=chunk["grouped"][:, cols, :].rearrange("p (c i) j -> p c j i", i=RUN),
                in_=chunk["rows"][:, :, cols].rearrange("p j (c i) -> p c j i", i=RUN),
            )

        def regroup_channels(copy, chunk, ms):
            copy(
                out=chunk["grouped"][:].rearrange("p (t m) j -> p m j t", t=PACK)[:, ms],
                in_=chunk["rows"][:].rearrange("p j (m t) -> p m j t", t=PACK)[:, ms],
            )

        def regroup_nf(chunk):
            regroup_channels(nc.scalar.copy, chunk, slice(0, SCALAR_COLS // PACK))
            regroup_channels(nc.vector.tensor_copy, chunk, slice(SCALAR_COLS // PACK, P))

        def regroup(chunk):
            regroup_columns(nc.scalar.copy, chunk, slice(0, SCALAR_COLS))
            regroup_columns(nc.vector.tensor_copy, chunk, slice(SCALAR_COLS, WIDTH))

        def quantise(chunk):
            nc.vector.quantize_mx(
                out=chunk["codes"][:].bitcast(FP8X4),
                scales=chunk["scales"][:],
                in_=chunk["grouped"][:].rearrange("p w j -> p (w j)"),
            )

        logit_rows = small_pool.tile([P, P], BF16)
        bias_rows = small_pool.tile([P, N_CH], BF16)
        ones_bf = small_pool.tile([P, P], BF16)
        ones_f32 = small_pool.tile([P, P], F32)
        ident_bf = small_pool.tile([P, P], BF16)
        neg_ident = small_pool.tile([P, P], BF16)
        table_warm = small_pool.tile([P, 1], F32)

        part_max_bf = small_pool.tile([P, 1], BF16)
        neg_max = small_pool.tile([P, 1], F32)
        exp_col = small_pool.tile([P, EDGE_TILES], F32)
        exp_part = small_pool.tile([P, 1], F32)
        inv_sum = small_pool.tile([P, 1], F32)
        attn_col = small_pool.tile([P, EDGE_TILES], F32)
        setup_banks = {}

        def softmax_partial_max():
            logit_ps = main_psum.tile([P, P], BF16, tag="lin", name="logit_ps")
            setup_banks["logits"] = logit_ps[:, 0:EDGE_TILES]
            nc.tensor.transpose(logit_ps[:], logit_rows[:], ident_bf[:])
            nc.vector.tensor_reduce(
                out=part_max_bf[:], in_=setup_banks["logits"], axis=AXIS.X, op=ALU.max
            )
            max_ps = main_psum.tile([P, P], F32, tag="lin", name="max_ps")
            setup_banks["max"] = max_ps
            nc.tensor.matmul(
                out=max_ps[:],
                lhsT=part_max_bf[:, 0:1].to_broadcast([P, P]),
                rhs=neg_ident[:],
                start=True,
                stop=True,
            )

        def softmax_max():
            nc.vector.tensor_reduce(
                out=neg_max[:], in_=setup_banks["max"][:], axis=AXIS.X, op=ALU.min
            )

        def softmax_exp():
            nc.scalar.activation(
                out=exp_col[:],
                in_=setup_banks["logits"],
                func=ACT.Exp,
                bias=neg_max[:, 0:1],
                accum_out=exp_part[:],
            )

        def softmax_sum():
            sum_ps = main_psum.tile([P, 1], F32, tag="lin", name="sum_ps")
            setup_banks["sum"] = sum_ps
            nc.tensor.matmul(out=sum_ps[:], lhsT=ones_f32[:], rhs=exp_part[:], start=True, stop=True)

        def softmax_normalise():
            nc.vector.reciprocal(out=inv_sum[:], in_=setup_banks["sum"][:])
            nc.gpsimd.tensor_scalar(
                out=attn_col[:],
                in0=exp_col[:],
                scalar1=inv_sum[:, 0:1],
                scalar2=0.0,
                op0=ALU.mult,
                op1=ALU.add,
            )

        bias_all = small_pool.tile([P, N_CH], F32)
        bias_attn = small_pool.tile([P, EDGE_TILES, N_CH], F32)

        def spread_bias():
            bias_ps = main_psum.tile([P, N_CH], F32, tag="lin", name="bias_ps")
            nc.tensor.matmul(out=bias_ps[:], lhsT=ones_bf[:], rhs=bias_rows[:], start=True, stop=True)
            setup_banks["bias"] = bias_ps

        def keep_bias():
            nc.scalar.copy(out=bias_all[:], in_=setup_banks["bias"][:])

        def scale_bias_on_scalar(i):
            nc.scalar.activation(
                out=bias_attn[:, i, :], in_=bias_all[:], func=ACT.Copy, scale=attn_col[:, i : i + 1]
            )

        def scale_bias_on_vector(i):
            nc.vector.tensor_scalar(
                out=bias_attn[:, i, :],
                in0=bias_all[:],
                scalar1=attn_col[:, i : i + 1],
                scalar2=None,
                op0=ALU.mult,
            )

        agg_grouped = agg_pool.tile([P, EDGE_TILES, P, PACK], BF16, align_bytes=64)
        agg_codes = agg_pool.tile([P, EDGE_TILES, P], U32, align_bytes=64)
        agg_scales = agg_pool.tile([P, EDGE_TILES, P], U8, align_bytes=64)
        agg_banks = {}
        lin_banks = {}

        def aggregate(h, c):
            for e in range(HALF):
                i = h * HALF + e
                if c == 0:
                    agg_banks[i] = main_psum.tile(
                        [P, CH_TILES, P], F32, tag="agg", name="agg_ps%d" % i, bufs=AGG_BANKS
                    )
                edges = slice(e * P, (e + 1) * P)
                for t in range(CH_TILES):
                    channels = slice(t * P, (t + 1) * P)
                    nc.tensor.matmul_mx(
                        out=agg_banks[i][:, t, :],
                        lhsT=nf[c]["codes"][:, channels].bitcast(FP8X4),
                        lhsT_scale=nf[c]["scales"][:, channels],
                        rhs=inc[h][c]["codes"][:, edges].bitcast(FP8X4),
                        rhs_scale=inc[h][c]["scales"][:, edges],
                        start=(c == 0 and t == 0),
                        stop=(c == NODE_PASSES - 1 and t == CH_TILES - 1),
                    )

        def warm_tensor(chunk):
            for j in range(2):
                scratch = main_psum.tile([P, WIDTH], F32, tag="lin", name="scratch")
                nc.tensor.matmul(
                    out=scratch[:], lhsT=ones_bf[:], rhs=chunk["rows"][:, j, :], start=True, stop=True
                )

        def round_agg(i):
            nc.scalar.copy(out=agg_grouped[:, i], in_=agg_banks[i][:].rearrange("p t e -> p e t"))

        def quantise_agg(i):
            nc.vector.quantize_mx(
                out=agg_codes[:, i, :].bitcast(FP8X4),
                scales=agg_scales[:, i, :],
                in_=agg_grouped[:, i].rearrange("p e t -> p (e t)"),
            )

        def project(i):
            lin_banks[i] = main_psum.tile([P, N_CH], F32, tag="lin", name="lin_ps%d" % i)
            nc.tensor.matmul_mx(
                out=lin_banks[i][:],
                lhsT=agg_codes[:, i, :].bitcast(FP8X4),
                lhsT_scale=agg_scales[:, i, :],
                rhs=w1["codes"][:].bitcast(FP8X4),
                rhs_scale=w1["scales"][:],
                start=True,
                stop=True,
            )

        def finish(i):
            result = result_pool.tile([P, N_CH], F32)
            nc.vector.scalar_tensor_tensor(
                out=result[:],
                in0=lin_banks[i][:],
                scalar=attn_col[:, i : i + 1],
                in1=bias_attn[:, i, :],
                op0=ALU.mult,
                op1=ALU.add,
            )
            nc.sync.dma_start(out=out[i * P : (i + 1) * P, :], in_=result[:])

        with tc.psum_pool(name="main_psum", bufs=LIN_BANKS) as main_psum, tc.manual_schedule():
            nc.vector.memset(table_warm[:], 0.0)
            nc.vector.memset(logit_rows[:], 0.0)
            nc.vector.memset(bias_rows[:], 0.0)
            nc.vector.memset(ones_bf[:], 1.0)
            nc.vector.memset(ones_f32[:], 1.0)
            make_identity(nc, ident_bf[:])
            nc.gpsimd.tensor_scalar(
                out=neg_ident[:], in0=ident_bf[:], scalar1=-1.0, scalar2=0.0, op0=ALU.mult, op1=ALU.add
            )
            nc.scalar.activation(out=table_warm[:], in_=table_warm[:], func=ACT.Exp)

            def load_nf(c):
                return load_chunk(
                    "nf%d" % c,
                    node_features[c * K_PASS : (c + 1) * K_PASS, :].rearrange("(p j) w -> p j w", j=PACK),
                )

            def load_inc(h):
                return [
                    load_chunk(
                        "inc%d_%d" % (h, c),
                        incidence[c * K_PASS : (c + 1) * K_PASS, h * WIDTH : (h + 1) * WIDTH].rearrange(
                            "(p j) w -> p j w", j=PACK
                        ),
                    )
                    for c in range(NODE_PASSES)
                ]

            nf = [load_nf(0)]
            nc.sync.dma_start(
                out=logit_rows[0:EDGE_TILES, :],
                in_=edge_attention.rearrange("(i q) -> i q", q=P),
            )
            nf += [load_nf(c) for c in range(1, NODE_PASSES)]
            nc.sync.dma_start(out=bias_rows[0:1, :], in_=b1.rearrange("(o n) -> o n", o=1))
            inc = [load_inc(0)]
            w1 = load_chunk("w1", W1.rearrange("(p t) n -> p t n", t=PACK))
            inc.append(load_inc(1))

            regroup_nf(nf[0])
            regroup_nf(nf[1])
            quantise(nf[0])
            softmax_partial_max()
            regroup_nf(nf[2])
            quantise(nf[1])
            softmax_max()
            regroup_nf(nf[3])
            softmax_exp()
            spread_bias()
            softmax_sum()
            quantise(nf[2])
            regroup(inc[0][0])
            keep_bias()
            softmax_normalise()
            warm_tensor(inc[0][0])
            quantise(nf[3])
            warm_tensor(inc[0][1])
            warm_tensor(inc[0][2])
            for c in range(1, NODE_PASSES):
                regroup(inc[0][c])
                quantise(inc[0][c - 1])
                aggregate(0, c - 1)
                if c > 1:
                    scale_bias_on_vector(c)
            regroup(w1)
            quantise(inc[0][NODE_PASSES - 1])
            aggregate(0, NODE_PASSES - 1)
            regroup(inc[1][0])
            quantise(w1)
            scale_bias_on_scalar(0)
            scale_bias_on_scalar(1)
            round_agg(0)
            for c in range(1, NODE_PASSES):
                regroup(inc[1][c])
                quantise_agg(c - 1)
                project(c - 1)
                round_agg(c)
                quantise(inc[1][c - 1])
                aggregate(1, c - 1)
                if c > 1:
                    finish(c - 2)
            quantise_agg(HALF - 1)
            project(HALF - 1)
            quantise(inc[1][NODE_PASSES - 1])
            aggregate(1, NODE_PASSES - 1)
            for i in range(HALF, EDGE_TILES - 1):
                scale_bias_on_scalar(i)
            for i in range(HALF, EDGE_TILES):
                if i == EDGE_TILES - 1:
                    scale_bias_on_scalar(i)
                round_agg(i)
            finish(HALF - 2)
            finish(HALF - 1)
            for i in range(HALF, EDGE_TILES):
                quantise_agg(i)
                project(i)
                if i > HALF:
                    finish(i - 1)
            finish(EDGE_TILES - 1)
